import numpy as np
import ml_dtypes


def mxq(x, axis, fmt="e4m3"):
    dtype, down = {"e4m3": (ml_dtypes.float8_e4m3fn, 7), "e5m2": (ml_dtypes.float8_e5m2, 14)}[fmt]
    v = np.moveaxis(np.asarray(x, np.float32).astype(ml_dtypes.bfloat16).astype(np.float64), axis, -1)
    blocks = v.reshape(v.shape[:-1] + (-1, 32))
    amax = np.abs(blocks).max(-1, keepdims=True)
    byte = np.maximum(np.where(amax > 0, np.frexp(amax)[1] - 1 + 127, 0) - down, 1)
    scale = np.exp2(byte - 127.0)
    codes = (blocks / scale).astype(np.float32).astype(dtype).astype(np.float64)
    return np.moveaxis((codes * scale).reshape(v.shape), -1, axis)


WIDE = False


def mx_kscale(k):
    if not WIDE:
        return np.ones(k)
    levels = np.array([18, -18])
    if k % 512:
        return np.exp2(np.random.permutation(np.resize(levels, k // 32))).repeat(32)
    a = np.empty((k // 512, 16))
    for p in range(k // 512):
        a[p, :8] = np.random.permutation(np.resize(levels, 8))
        for g in range(8):
            far = levels[np.abs(levels - a[p, g]) >= 10]
            a[p, g + 8] = far[np.random.randint(len(far))]
    return np.exp2(a.ravel()).repeat(32)


BF16 = ml_dtypes.bfloat16


def bf(x):
    return np.asarray(x, np.float32).astype(BF16)


def f64(x):
    return np.asarray(x).astype(np.float64)


NB, S, DI, DO, R = 4, 128, 2048, 2048, 512
T = NB * S
SCALE = 0.125


def setup_inputs():
    s = mx_kscale(T).reshape(NB, S, 1)
    u = mx_kscale(DO)
    v = mx_kscale(R)
    x0 = bf(np.random.standard_normal((NB, S, DI)))
    A0 = bf(np.random.standard_normal((R, DI)) * 3.0 / np.sqrt(DI))
    B0 = bf(np.random.standard_normal((DO, R)) * 3.0 / np.sqrt(R))
    d_A = bf(1.0 + 0.1 * np.random.standard_normal(R))
    d_B = bf(np.random.standard_normal(DO))
    g = bf(2.0 * np.random.standard_normal((NB, S, DO)) * np.exp2(np.random.randint(-6, 1, (NB, S, 1))) / s * u)
    z1 = f64(x0) @ f64(A0).T
    return {"x": bf(f64(x0) * s),
            "A": bf(f64(A0) / v[:, None]),
            "B": bf(f64(B0) * v / u[:, None]),
            "d_A": d_A,
            "d_B": d_B,
            "z1": np.asarray(z1, np.float32),
            "grad_out": g}


def reference(x, A, B, d_A, d_B, z1, grad_out):
    xf = f64(x).reshape(T, DI)
    dz2 = f64(grad_out).reshape(T, DO) * f64(d_B) * SCALE
    dh = mxq(dz2, 1, "e5m2") @ mxq(f64(B), 0, "e4m3")
    dz1 = dh * f64(d_A)
    dx = mxq(dz1, 1, "e5m2") @ mxq(f64(A), 0, "e4m3")
    dA = mxq(dz1, 0, "e5m2").T @ mxq(xf, 0, "e4m3")
    return dx.reshape(NB, S, DI), dA

@@ -1,0 +1,310 @@
+from contextlib import ExitStack
+
+import concourse.mybir as mybir
+from concourse.masks import make_identity
+
+T, DI, DO, R = 512, 2048, 2048, 512
+P = 128
+PASSES = DO // 512
+SCALE = 0.125
+
+FLOPS = 3 * 2 * T * DO * R
+BYTES = 2 * (T * DI + R * DI + DO * R + T * DO + R + DO) + 4 * (T * DI + R * DI)
+
+F32 = mybir.dt.float32
+BF16 = mybir.dt.bfloat16
+U32 = mybir.dt.uint32
+U8 = mybir.dt.uint8
+E4M3 = mybir.dt.float8_e4m3fn_x4
+E5M2 = mybir.dt.float8_e5m2_x4
+COPY = mybir.ActivationFunctionType.Copy
+MULT = mybir.AluOpType.mult
+
+
+def tile_veralayer_pa_v_kernel(tc, x, A, B, d_A, d_B, z1, grad_out, out_0, out_1):
+    nc = tc.nc
+    with ExitStack() as ctx:
+        keep = ctx.enter_context(tc.tile_pool(name="keep", bufs=1))
+        stage = ctx.enter_context(tc.tile_pool(name="stage", bufs=6))
+        psum = ctx.enter_context(tc.psum_pool(name="psum", bufs=8))
+        ctx.enter_context(tc.manual_schedule())
+
+        def sb(name, shape, dtype):
+            return keep.tile(shape, dtype, name=name, align_bytes=64)
+
+        ident = sb("ident", [P, P], F32)
+        warm = sb("warm", [P, 8], F32)
+        db_raw = sb("db_raw", [P, PASSES, 4], BF16)
+        db = sb("db", [P, PASSES, 4], BF16)
+        da_raw = sb("da_raw", [P, 4], BF16)
+        da = sb("da", [P, 4], F32)
+        g_raw = [[sb("g_raw%d%d" % (f, jj), [P, 2, 1024], BF16) for jj in range(2)] for f in range(2)]
+        b_raw = [sb("b_raw%d" % g, [P, 4, R], BF16) for g in range(PASSES)]
+        a_raw = [sb("a_raw%d" % h, [P, 4, 1024], BF16) for h in range(2)]
+        x_raw = sb("x_raw", [P, 4, DI], BF16)
+        dz2_g = sb("dz2_g", [P, PASSES, T, 4], BF16)
+        dz2_c = sb("dz2_c", [P, PASSES, T], U32)
+        dz2_s = sb("dz2_s", [P, PASSES, T], U8)
+        b_g = [sb("b_g%d" % g, [P, R, 4], BF16) for g in range(PASSES)]
+        b_c = sb("b_c", [P, PASSES, R], U32)
+        b_s = sb("b_s", [P, PASSES, R], U8)
+        w_g = [sb("w_g%d" % k, [P, 512, 4], BF16) for k in range(3)]
+        a_c = sb("a_c", [P, DI], U32)
+        a_s = sb("a_s", [P, DI], U8)
+        x_c = sb("x_c", [P, DI], U32)
+        x_s = sb("x_s", [P, DI], U8)
+        d_t = sb("d_t", [P, 4, T], BF16)
+        dr_g = sb("dr_g", [P, T, 4], BF16)
+        dr_c = sb("dr_c", [P, T], U32)
+        dr_s = sb("dr_s", [P, T], U8)
+        dt_g = sb("dt_g", [P, R, 4], BF16)
+        dt_c = sb("dt_c", [P, R], U32)
+        dt_s = sb("dt_s", [P, R], U8)
+
+        nc.scalar.dma_start(out=db_raw[:], in_=d_B.rearrange("(g p j) -> p g j", p=P, j=4))
+        nc.scalar.dma_start(out=da_raw[:], in_=d_A.rearrange("(p j) -> p j", j=4))
+
+        g_v = grad_out.rearrange("b s w -> s b w")
+
+        def load_g(f, jj):
+            nc.sync.dma_start(out=g_raw[f][jj][:], in_=g_v[:, 2 * jj : 2 * jj + 2, 1024 * f : 1024 * (f + 1)])
+
+        def load_b(g):
+            nc.sync.dma_start(out=b_raw[g][:], in_=B[512 * g : 512 * (g + 1), :].rearrange("(p j) r -> p j r", j=4))
+
+        load_b(0)
+        load_g(0, 0)
+        load_g(0, 1)
+        load_b(1)
+        load_g(1, 0)
+        load_b(2)
+        load_g(1, 1)
+        load_b(3)
+        a_v = A.rearrange("(p j) w -> p j w", j=4)
+        for h in range(2):
+            nc.sync.dma_start(out=a_raw[h][:], in_=a_v[:, :, 1024 * h : 1024 * (h + 1)])
+        x_v = x.rearrange("b s w -> (b s) w").rearrange("(p j) w -> p j w", j=4)
+        for h in range(2):
+            nc.sync.dma_start(out=x_raw[:, 2 * h : 2 * h + 2, :], in_=x_v[:, 2 * h : 2 * h + 2, :])
+
+        make_identity(nc, ident[:])
+        nc.vector.memset(warm[:, 0:4], 0.0)
+        nc.scalar.copy(out=warm[:, 4:5], in_=warm[:, 0:1])
+        nc.gpsimd.tensor_scalar(out=db[:], in0=db_raw[:], scalar1=SCALE, scalar2=None, op0=MULT)
+        nc.gpsimd.tensor_copy(out=da[:], in_=da_raw[:])
+
+        def copy(eng, out, in_):
+            if eng == "v":
+                nc.vector.tensor_copy(out=out, in_=in_)
+            else:
+                nc.scalar.copy(out=out, in_=in_)
+
+        def il_b(eng, g, m0, m1):
+            copy(
+                eng,
+                b_g[g][:].rearrange("p (t m) j -> p m t j", t=4)[:, m0:m1],
+                b_raw[g][:].rearrange("p j (m t) -> p m t j", t=4)[:, m0:m1],
+            )
+
+        def q_b(g):
+            nc.vector.quantize_mx(
+                out=b_c[:, g, :].bitcast(E4M3), scales=b_s[:, g, :], in_=b_g[g][:].rearrange("p c j -> p (c j)")
+            )
+
+        def bank():
+            return psum.tile([P, 512], F32, name="bank")
+
+        def tr_g(f, jj):
+            banks = [bank() for gl in range(2)]
+            for k in range(2):
+                words = g_raw[f][jj][:, k, :].bitcast(F32)
+                for gl in range(2):
+                    for u in range(2):
+                        c0 = 256 * u + 128 * k
+                        nc.tensor.transpose(
+                            banks[gl][:, c0 : c0 + 128], words[:, 256 * gl + u : 256 * (gl + 1) : 2], ident[:]
+                        )
+            return banks
+
+        def evac_g(f, jj, banks):
+            for gl in range(2):
+                g = 2 * f + gl
+                nc.vector.tensor_tensor(
+                    out=dz2_g[:, g, 256 * jj : 256 * (jj + 1), :].rearrange("p r (u e) -> p r u e", u=2),
+                    in0=banks[gl][:].bitcast(BF16).rearrange("p (u r e) -> p r u e", u=2, e=2),
+                    in1=db[:, g, :].rearrange("p (u e) -> p u e", u=2).unsqueeze(1).to_broadcast([P, 256, 2, 2]),
+                    op=MULT,
+                )
+
+        def q_g(g):
+            nc.vector.quantize_mx(
+                out=dz2_c[:, g, :].bitcast(E5M2),
+                scales=dz2_s[:, g, :],
+                in_=dz2_g[:, g, :, :].rearrange("p c j -> p (c j)"),
+            )
+
+        def mx_dh(g):
+            for t in range(4):
+                nc.tensor.matmul_mx(
+                    out=acc[t][:],
+                    lhsT=b_c[:, g, 128 * t : 128 * (t + 1)].bitcast(E4M3),
+                    lhsT_scale=b_s[:, g, 128 * t : 128 * (t + 1)],
+                    rhs=dz2_c[:, g, :].bitcast(E5M2),
+                    rhs_scale=dz2_s[:, g, :],
+                    start=(g == 0),
+                    stop=(g == PASSES - 1),
+                )
+
+        def il(eng, dst, src):
+            copy(eng, dst.rearrange("p (c i) t -> p c t i", i=4), src.rearrange("p t (c i) -> p c t i", i=4))
+
+        def il_w(eng, k, c0=0, c1=512):
+            if k < 4:
+                src = a_raw[k // 2][:, :, 512 * (k % 2) + c0 : 512 * (k % 2) + c1]
+            else:
+                src = x_raw[:, :, 512 * (k - 4) + c0 : 512 * (k - 4) + c1]
+            il(eng, w_g[k % 3][:, c0:c1, :], src)
+
+        def q_w(k):
+            c, s = (a_c, a_s) if k < 4 else (x_c, x_s)
+            cols = slice(512 * (k % 4), 512 * (k % 4 + 1))
+            nc.vector.quantize_mx(
+                out=c[:, cols].bitcast(E4M3), scales=s[:, cols], in_=w_g[k % 3][:].rearrange("p c j -> p (c j)")
+            )
+
+        def q_dr(h):
+            cols = slice(256 * h, 256 * (h + 1))
+            nc.vector.quantize_mx(
+                out=dr_c[:, cols].bitcast(E5M2), scales=dr_s[:, cols], in_=dr_g[:, cols, :].rearrange("p c j -> p (c j)")
+            )
+
+
+        il_b("v", 0, 0, 64)
+        il_b("s", 0, 64, 128)
+        bl0 = tr_g(0, 0)
+        bl1 = tr_g(0, 1)
+        evac_g(0, 0, bl0)
+        q_b(0)
+        evac_g(0, 1, bl1)
+        il_b("s", 1, 0, 128)
+        br0 = tr_g(1, 0)
+        q_g(0)
+        q_g(1)
+        acc = [bank() for t in range(4)]
+        evac_g(1, 0, br0)
+        q_b(1)
+        mx_dh(0)
+        il_b("s", 2, 0, 128)
+        br1 = tr_g(1, 1)
+        mx_dh(1)
+        evac_g(1, 1, br1)
+        il_b("v", 3, 0, 64)
+        il_b("s", 3, 64, 128)
+        q_g(2)
+        q_b(2)
+        mx_dh(2)
+        q_g(3)
+        q_b(3)
+        mx_dh(3)
+        il_w("v", 0, 0, 256)
+        il_w("s", 0, 256, 512)
+        for t in range(4):
+            if t % 2 == 0:
+                nc.scalar.activation(out=d_t[:, t, :], in_=acc[t][:], func=COPY, scale=da[:, t : t + 1])
+            else:
+                nc.vector.tensor_scalar(
+                    out=d_t[:, t, :], in0=acc[t][:], scalar1=da[:, t : t + 1], scalar2=None, op0=MULT
+                )
+        il("v", dr_g[:, 0:256, :], d_t[:, :, 0:256])
+        il("s", dr_g[:, 256:512, :], d_t[:, :, 256:512])
+        q_w(0)
+        q_dr(0)
+        q_dr(1)
+
+        def tr_d():
+            banks = [bank() for k in range(2)]
+            words = d_t[:].rearrange("p t r -> p (t r)").bitcast(F32)
+            for k in range(2):
+                for u in range(2):
+                    for i in range(2):
+                        t = 2 * k + i
+                        c0 = 256 * u + 128 * i
+                        nc.tensor.transpose(
+                            banks[k][:, c0 : c0 + 128], words[:, 256 * t + u : 256 * (t + 1) : 2], ident[:]
+                        )
+            return banks
+
+        def evac_d(banks, k):
+            nc.vector.tensor_copy(
+                out=dt_g[:, 256 * k : 256 * (k + 1), :].rearrange("p c j -> p (c j)").bitcast(F32).rearrange("p (c u) -> p c u", u=2),
+                in_=banks[k][:].rearrange("p (u c) -> p c u", u=2),
+            )
+
+        def q_dt():
+            nc.vector.quantize_mx(out=dt_c[:].bitcast(E5M2), scales=dt_s[:], in_=dt_g[:].rearrange("p c j -> p (c j)"))
+
+        def mx_out(ps, chunk, mt):
+            lc, ls = (dr_c, dr_s) if chunk < 4 else (dt_c, dt_s)
+            rc, rs = (a_c, a_s) if chunk < 4 else (x_c, x_s)
+            rows = slice(128 * mt, 128 * (mt + 1))
+            cols = slice(512 * (chunk % 4), 512 * (chunk % 4 + 1))
+            nc.tensor.matmul_mx(
+                out=ps[:],
+                lhsT=lc[:, rows].bitcast(E5M2),
+                lhsT_scale=ls[:, rows],
+                rhs=rc[:, cols].bitcast(E4M3),
+                rhs_scale=rs[:, cols],
+                start=True,
+                stop=True,
+            )
+
+        out0_v = out_0.rearrange("b s w -> s b w")
+        out1_v = out_1.rearrange("(m t) n -> m t n", t=4)
+        on_vector = {27, 29, 31}
+        dbanks = []
+
+        def vector_work(n):
+            if n == 1:
+                il_w("v", 1)
+            elif n == 3:
+                q_w(1)
+                dbanks.extend(tr_d())
+                il_w("v", 2)
+            elif n == 5:
+                evac_d(dbanks, 0)
+                q_w(2)
+                il_w("v", 3)
+            elif n == 9:
+                evac_d(dbanks, 1)
+                q_w(3)
+                il_w("v", 4)
+                q_dt()
+            elif n == 13:
+                q_w(4)
+                il_w("v", 5)
+            elif n == 17:
+                q_w(5)
+                il_w("v", 6)
+            elif n == 21:
+                q_w(6)
+                il_w("v", 7)
+            elif n == 25:
+                q_w(7)
+
+        for chunk in range(8):
+            cols = slice(512 * (chunk % 4), 512 * (chunk % 4 + 1))
+            view = out0_v if chunk < 4 else out1_v
+            for q in range(2):
+                st = stage.tile([P, 2, 512], F32, name="st")
+                for i in range(2):
+                    mt = 2 * q + i
+                    n = 4 * chunk + mt
+                    ps = bank()
+                    mx_out(ps, chunk, mt)
+                    copy("v" if n in on_vector else "s", st[:, i, :], ps[:])
+                    if n == 31:
+                        for k in range(2):
+                            nc.sync.dma_start(out=view[:, 2 + k, cols], in_=st[:, k, :])
+                    vector_work(n)
+                if n != 31:
+                    nc.sync.dma_start(out=view[:, 2 * q : 2 * q + 2, cols], in_=st[:])

@@ -7,6 +7,7 @@ T, DI, DO, R = 512, 2048, 2048, 512
 P = 128
 PASSES = DO // 512
 SCALE = 0.125
+ND = (8, 3, 3, 3, 0)
 
 FLOPS = 3 * 2 * T * DO * R
 BYTES = 2 * (T * DI + R * DI + DO * R + T * DO + R + DO) + 4 * (T * DI + R * DI)
@@ -26,7 +27,7 @@ def tile_veralayer_pa_v_kernel(tc, x, A, B, d_A, d_B, z1, grad_out, out_0, out_1
     with ExitStack() as ctx:
         keep = ctx.enter_context(tc.tile_pool(name="keep", bufs=1))
         stage = ctx.enter_context(tc.tile_pool(name="stage", bufs=6))
-        psum = ctx.enter_context(tc.psum_pool(name="psum", bufs=8))
+        psum = ctx.enter_context(tc.psum_pool(name="psum", bufs=7))
         ctx.enter_context(tc.manual_schedule())
 
         def sb(name, shape, dtype):
@@ -34,9 +35,10 @@ def tile_veralayer_pa_v_kernel(tc, x, A, B, d_A, d_B, z1, grad_out, out_0, out_1
 
         ident = sb("ident", [P, P], F32)
         warm = sb("warm", [P, 8], F32)
-        db_raw = sb("db_raw", [P, PASSES, 4], BF16)
+        zero = sb("zero", [P, 512], BF16)
+        vec_raw = sb("vec_raw", [P, 512], BF16)
+        vec = sb("vec", [P, 512], F32)
         db = sb("db", [P, PASSES, 4], BF16)
-        da_raw = sb("da_raw", [P, 4], BF16)
         da = sb("da", [P, 4], F32)
         g_raw = [[sb("g_raw%d%d" % (f, jj), [P, 2, 1024], BF16) for jj in range(2)] for f in range(2)]
         b_raw = [sb("b_raw%d" % g, [P, 4, R], BF16) for g in range(PASSES)]
@@ -61,9 +63,6 @@ def tile_veralayer_pa_v_kernel(tc, x, A, B, d_A, d_B, z1, grad_out, out_0, out_1
         dt_c = sb("dt_c", [P, R], U32)
         dt_s = sb("dt_s", [P, R], U8)
 
-        nc.scalar.dma_start(out=db_raw[:], in_=d_B.rearrange("(g p j) -> p g j", p=P, j=4))
-        nc.scalar.dma_start(out=da_raw[:], in_=d_A.rearrange("(p j) -> p j", j=4))
-
         g_v = grad_out.rearrange("b s w -> s b w")
 
         def load_g(f, jj):
@@ -72,8 +71,12 @@ def tile_veralayer_pa_v_kernel(tc, x, A, B, d_A, d_B, z1, grad_out, out_0, out_1
         def load_b(g):
             nc.sync.dma_start(out=b_raw[g][:], in_=B[512 * g : 512 * (g + 1), :].rearrange("(p j) r -> p j r", j=4))
 
-        load_b(0)
+        nc.gpsimd.memset(vec_raw[:].bitcast(U32), 0)
+        nc.vector.memset(zero[:], 0.0)
+        nc.sync.dma_start(out=vec_raw[0:4, :], in_=d_B.rearrange("(g w) -> g w", g=4))
+        nc.sync.dma_start(out=vec_raw[4:5, :], in_=d_A.rearrange("(g w) -> g w", g=1))
         load_g(0, 0)
+        load_b(0)
         load_g(0, 1)
         load_b(1)
         load_g(1, 0)
@@ -81,17 +84,15 @@ def tile_veralayer_pa_v_kernel(tc, x, A, B, d_A, d_B, z1, grad_out, out_0, out_1
         load_g(1, 1)
         load_b(3)
         a_v = A.rearrange("(p j) w -> p j w", j=4)
+        x_v = x.rearrange("b s w -> (b s) w").rearrange("(p j) w -> p j w", j=4)
         for h in range(2):
             nc.sync.dma_start(out=a_raw[h][:], in_=a_v[:, :, 1024 * h : 1024 * (h + 1)])
-        x_v = x.rearrange("b s w -> (b s) w").rearrange("(p j) w -> p j w", j=4)
         for h in range(2):
             nc.sync.dma_start(out=x_raw[:, 2 * h : 2 * h + 2, :], in_=x_v[:, 2 * h : 2 * h + 2, :])
 
         make_identity(nc, ident[:])
         nc.vector.memset(warm[:, 0:4], 0.0)
         nc.scalar.copy(out=warm[:, 4:5], in_=warm[:, 0:1])
-        nc.gpsimd.tensor_scalar(out=db[:], in0=db_raw[:], scalar1=SCALE, scalar2=None, op0=MULT)
-        nc.gpsimd.tensor_copy(out=da[:], in_=da_raw[:])
 
         def copy(eng, out, in_):
             if eng == "v":
@@ -102,8 +103,8 @@ def tile_veralayer_pa_v_kernel(tc, x, A, B, d_A, d_B, z1, grad_out, out_0, out_1
         def il_b(eng, g, m0, m1):
             copy(
                 eng,
-                b_g[g][:].rearrange("p (t m) j -> p m t j", t=4)[:, m0:m1],
-                b_raw[g][:].rearrange("p j (m t) -> p m t j", t=4)[:, m0:m1],
+                b_g[g][:].rearrange("p (t m) j -> p t m j", t=4)[:, :, m0:m1],
+                b_raw[g][:].rearrange("p j (m t) -> p t m j", t=4)[:, :, m0:m1],
             )
 
         def q_b(g):
@@ -114,11 +115,27 @@ def tile_veralayer_pa_v_kernel(tc, x, A, B, d_A, d_B, z1, grad_out, out_0, out_1
         def bank():
             return psum.tile([P, 512], F32, name="bank")
 
+        dbank = psum.tile([P, 512], F32, name="dbank", bufs=1)
+
+        def dummies(count):
+            for k in range(count):
+                nc.tensor.matmul(dbank[:], lhsT=zero[:, 0:128], rhs=zero[:], start=True, stop=True)
+
+        dummies(ND[0])
+
+        nc.vector.tensor_copy(out=vec[:], in_=vec_raw[:])
+        vbank = bank()
+        for j in range(4):
+            nc.tensor.transpose(vbank[:, 128 * j : 128 * (j + 1)], vec[:, j:512:4], ident[:])
+        vview = vbank[:].rearrange("p (j r) -> p r j", j=4)
+        nc.vector.tensor_scalar(out=db[:], in0=vview[:, 0:4, :], scalar1=SCALE, scalar2=None, op0=MULT)
+        nc.vector.tensor_copy(out=da[:], in_=vview[:, 4, :])
+
         def tr_g(f, jj):
             banks = [bank() for gl in range(2)]
-            for k in range(2):
-                words = g_raw[f][jj][:, k, :].bitcast(F32)
-                for gl in range(2):
+            for gl in range(2):
+                for k in range(2):
+                    words = g_raw[f][jj][:, k, :].bitcast(F32)
                     for u in range(2):
                         c0 = 256 * u + 128 * k
                         nc.tensor.transpose(
@@ -159,11 +176,9 @@ def tile_veralayer_pa_v_kernel(tc, x, A, B, d_A, d_B, z1, grad_out, out_0, out_1
             copy(eng, dst.rearrange("p (c i) t -> p c t i", i=4), src.rearrange("p t (c i) -> p c t i", i=4))
 
         def il_w(eng, k, c0=0, c1=512):
-            if k < 4:
-                src = a_raw[k // 2][:, :, 512 * (k % 2) + c0 : 512 * (k % 2) + c1]
-            else:
-                src = x_raw[:, :, 512 * (k - 4) + c0 : 512 * (k - 4) + c1]
-            il(eng, w_g[k % 3][:, c0:c1, :], src)
+            raw = a_raw[k // 2] if k < 4 else x_raw
+            base = 512 * (k % 2) if k < 4 else 512 * (k - 4)
+            il(eng, w_g[k % 3][:, c0:c1, :], raw[:, :, base + c0 : base + c1])
 
         def q_w(k):
             c, s = (a_c, a_s) if k < 4 else (x_c, x_s)
@@ -178,47 +193,50 @@ def tile_veralayer_pa_v_kernel(tc, x, A, B, d_A, d_B, z1, grad_out, out_0, out_1
                 out=dr_c[:, cols].bitcast(E5M2), scales=dr_s[:, cols], in_=dr_g[:, cols, :].rearrange("p c j -> p (c j)")
             )
 
-
-        il_b("v", 0, 0, 64)
-        il_b("s", 0, 64, 128)
         bl0 = tr_g(0, 0)
-        bl1 = tr_g(0, 1)
+        dummies(ND[1])
+        il_b("s", 0, 0, 128)
         evac_g(0, 0, bl0)
-        q_b(0)
+        bl1 = tr_g(0, 1)
+        dummies(ND[2])
         evac_g(0, 1, bl1)
+        q_b(0)
+        q_g(0)
         il_b("s", 1, 0, 128)
         br0 = tr_g(1, 0)
-        q_g(0)
+        dummies(ND[3])
         q_g(1)
-        acc = [bank() for t in range(4)]
         evac_g(1, 0, br0)
-        q_b(1)
-        mx_dh(0)
-        il_b("s", 2, 0, 128)
         br1 = tr_g(1, 1)
-        mx_dh(1)
+        dummies(ND[4])
+        q_b(1)
         evac_g(1, 1, br1)
-        il_b("v", 3, 0, 64)
-        il_b("s", 3, 64, 128)
+        acc = [bank() for t in range(4)]
+        mx_dh(0)
+        mx_dh(1)
+        il_b("s", 2, 0, 128)
+        il_b("s", 3, 0, 128)
         q_g(2)
+        q_g(3)
         q_b(2)
         mx_dh(2)
-        q_g(3)
         q_b(3)
         mx_dh(3)
-        il_w("v", 0, 0, 256)
         il_w("s", 0, 256, 512)
+        il_w("v", 0, 0, 256)
         for t in range(4):
-            if t % 2 == 0:
+            if t in (0, 2):
                 nc.scalar.activation(out=d_t[:, t, :], in_=acc[t][:], func=COPY, scale=da[:, t : t + 1])
             else:
                 nc.vector.tensor_scalar(
                     out=d_t[:, t, :], in0=acc[t][:], scalar1=da[:, t : t + 1], scalar2=None, op0=MULT
                 )
-        il("v", dr_g[:, 0:256, :], d_t[:, :, 0:256])
-        il("s", dr_g[:, 256:512, :], d_t[:, :, 256:512])
+        il("v", dr_g[:, 0:320, :], d_t[:, :, 0:320])
+        il("s", dr_g[:, 320:512, :], d_t[:, :, 320:512])
         q_w(0)
         q_dr(0)
+        il_w("v", 1, 0, 384)
+        il_w("s", 1, 384, 512)
         q_dr(1)
 
         def tr_d():
@@ -258,53 +276,69 @@ def tile_veralayer_pa_v_kernel(tc, x, A, B, d_A, d_B, z1, grad_out, out_0, out_1
                 stop=True,
             )
 
-        out0_v = out_0.rearrange("b s w -> s b w")
         out1_v = out_1.rearrange("(m t) n -> m t n", t=4)
-        on_vector = {27, 29, 31}
+        out0_v = out_0.rearrange("b s w -> s b w")
+        on_vector = {25, 27, 29, 31}
         dbanks = []
 
         def vector_work(n):
             if n == 1:
-                il_w("v", 1)
-            elif n == 3:
                 q_w(1)
-                dbanks.extend(tr_d())
                 il_w("v", 2)
-            elif n == 5:
-                evac_d(dbanks, 0)
+            elif n == 3:
                 q_w(2)
                 il_w("v", 3)
-            elif n == 9:
-                evac_d(dbanks, 1)
+            elif n == 5:
+                dbanks.extend(tr_d())
                 q_w(3)
+            elif n == 7:
+                evac_d(dbanks, 0)
+                evac_d(dbanks, 1)
                 il_w("v", 4)
                 q_dt()
-            elif n == 13:
+            elif n == 9:
                 q_w(4)
                 il_w("v", 5)
-            elif n == 17:
+            elif n == 13:
                 q_w(5)
                 il_w("v", 6)
-            elif n == 21:
+            elif n == 18:
                 q_w(6)
                 il_w("v", 7)
-            elif n == 25:
+            elif n == 21:
                 q_w(7)
 
-        for chunk in range(8):
-            cols = slice(512 * (chunk % 4), 512 * (chunk % 4 + 1))
-            view = out0_v if chunk < 4 else out1_v
-            for q in range(2):
+        def emit(n, chunk, mt, dst):
+            ps = bank()
+            mx_out(ps, chunk, mt)
+            copy("v" if n in on_vector else "s", dst, ps[:])
+            vector_work(n)
+
+        out0_v = out_0.rearrange("b s w -> s b w")
+        n = 0
+        for unit in range(4):
+            view = out0_v if unit < 2 else out1_v
+            c0 = 1024 * (unit % 2)
+            for q in range(4):
                 st = stage.tile([P, 2, 512], F32, name="st")
-                for i in range(2):
-                    mt = 2 * q + i
-                    n = 4 * chunk + mt
-                    ps = bank()
-                    mx_out(ps, chunk, mt)
-                    copy("v" if n in on_vector else "s", st[:, i, :], ps[:])
-                    if n == 31:
-                        for k in range(2):
-                            nc.sync.dma_start(out=view[:, 2 + k, cols], in_=st[:, k, :])
-                    vector_work(n)
-                if n != 31:
-                    nc.sync.dma_start(out=view[:, 2 * q : 2 * q + 2, cols], in_=st[:])
+                if unit % 2 == 0:
+                    chunk, m0 = 2 * unit + q // 2, 2 * (q % 2)
+                    cols = slice(c0 + 512 * (q // 2), c0 + 512 * (q // 2 + 1))
+                    for i in range(2):
+                        emit(n, chunk, m0 + i, st[:, i, :])
+                        n += 1
+                        if n <= 2:
+                            nc.sync.dma_start(out=view[:, m0 + i, cols], in_=st[:, i, :])
+                    if n > 2:
+                        nc.sync.dma_start(out=view[:, m0 : m0 + 2, cols], in_=st[:])
+                else:
+                    for i in range(2):
+                        emit(n, 2 * unit + i, q, st[:, i, :])
+                        n += 1
+                        if n > 30:
+                            cols = slice(c0 + 512 * i, c0 + 512 * (i + 1))
+                            nc.sync.dma_start(out=view[:, q, cols], in_=st[:, i, :])
+                    if n <= 30:
+                        nc.sync.dma_start(
+                            out=view[:, q, c0 : c0 + 1024], in_=st[:].rearrange("p i w -> p (i w)")
+                        )

@@ -7,7 +7,6 @@ T, DI, DO, R = 512, 2048, 2048, 512
 P = 128
 PASSES = DO // 512
 SCALE = 0.125
-ND = (8, 3, 3, 3, 0)
 
 FLOPS = 3 * 2 * T * DO * R
 BYTES = 2 * (T * DI + R * DI + DO * R + T * DO + R + DO) + 4 * (T * DI + R * DI)
@@ -27,7 +26,7 @@ def tile_veralayer_pa_v_kernel(tc, x, A, B, d_A, d_B, z1, grad_out, out_0, out_1
     with ExitStack() as ctx:
         keep = ctx.enter_context(tc.tile_pool(name="keep", bufs=1))
         stage = ctx.enter_context(tc.tile_pool(name="stage", bufs=6))
-        psum = ctx.enter_context(tc.psum_pool(name="psum", bufs=7))
+        psum = ctx.enter_context(tc.psum_pool(name="psum", bufs=8))
         ctx.enter_context(tc.manual_schedule())
 
         def sb(name, shape, dtype):
@@ -35,7 +34,6 @@ def tile_veralayer_pa_v_kernel(tc, x, A, B, d_A, d_B, z1, grad_out, out_0, out_1
 
         ident = sb("ident", [P, P], F32)
         warm = sb("warm", [P, 8], F32)
-        zero = sb("zero", [P, 512], BF16)
         vec_raw = sb("vec_raw", [P, 512], BF16)
         vec = sb("vec", [P, 512], F32)
         db = sb("db", [P, PASSES, 4], BF16)
@@ -71,17 +69,16 @@ def tile_veralayer_pa_v_kernel(tc, x, A, B, d_A, d_B, z1, grad_out, out_0, out_1
         def load_b(g):
             nc.sync.dma_start(out=b_raw[g][:], in_=B[512 * g : 512 * (g + 1), :].rearrange("(p j) r -> p j r", j=4))
 
-        nc.gpsimd.memset(vec_raw[:].bitcast(U32), 0)
-        nc.vector.memset(zero[:], 0.0)
+        nc.vector.memset(vec_raw[:], 0.0)
         nc.sync.dma_start(out=vec_raw[0:4, :], in_=d_B.rearrange("(g w) -> g w", g=4))
         nc.sync.dma_start(out=vec_raw[4:5, :], in_=d_A.rearrange("(g w) -> g w", g=1))
         load_g(0, 0)
         load_b(0)
         load_g(0, 1)
-        load_b(1)
         load_g(1, 0)
-        load_b(2)
+        load_b(1)
         load_g(1, 1)
+        load_b(2)
         load_b(3)
         a_v = A.rearrange("(p j) w -> p j w", j=4)
         x_v = x.rearrange("b s w -> (b s) w").rearrange("(p j) w -> p j w", j=4)
@@ -101,10 +98,11 @@ def tile_veralayer_pa_v_kernel(tc, x, A, B, d_A, d_B, z1, grad_out, out_0, out_1
                 nc.scalar.copy(out=out, in_=in_)
 
         def il_b(eng, g, m0, m1):
+            cut = (slice(None), slice(None), slice(m0, m1)) if eng == "v" else (slice(None), slice(m0, m1))
             copy(
                 eng,
-                b_g[g][:].rearrange("p (t m) j -> p t m j", t=4)[:, :, m0:m1],
-                b_raw[g][:].rearrange("p j (m t) -> p t m j", t=4)[:, :, m0:m1],
+                b_g[g][:].rearrange("p (t m) j -> p %s j" % ("t m" if eng == "v" else "m t"), t=4)[cut],
+                b_raw[g][:].rearrange("p j (m t) -> p %s j" % ("t m" if eng == "v" else "m t"), t=4)[cut],
             )
 
         def q_b(g):
@@ -114,14 +112,6 @@ def tile_veralayer_pa_v_kernel(tc, x, A, B, d_A, d_B, z1, grad_out, out_0, out_1
 
         def bank():
             return psum.tile([P, 512], F32, name="bank")
-
-        dbank = psum.tile([P, 512], F32, name="dbank", bufs=1)
-
-        def dummies(count):
-            for k in range(count):
-                nc.tensor.matmul(dbank[:], lhsT=zero[:, 0:128], rhs=zero[:], start=True, stop=True)
-
-        dummies(ND[0])
 
         nc.vector.tensor_copy(out=vec[:], in_=vec_raw[:])
         vbank = bank()
@@ -194,21 +184,18 @@ def tile_veralayer_pa_v_kernel(tc, x, A, B, d_A, d_B, z1, grad_out, out_0, out_1
             )
 
         bl0 = tr_g(0, 0)
-        dummies(ND[1])
-        il_b("s", 0, 0, 128)
+        il_b("s", 0, 64, 128)
         evac_g(0, 0, bl0)
+        il_b("v", 0, 0, 64)
         bl1 = tr_g(0, 1)
-        dummies(ND[2])
         evac_g(0, 1, bl1)
         q_b(0)
         q_g(0)
         il_b("s", 1, 0, 128)
         br0 = tr_g(1, 0)
-        dummies(ND[3])
         q_g(1)
         evac_g(1, 0, br0)
         br1 = tr_g(1, 1)
-        dummies(ND[4])
         q_b(1)
         evac_g(1, 1, br1)
         acc = [bank() for t in range(4)]

@@ -17,7 +17,6 @@ U32 = mybir.dt.uint32
 U8 = mybir.dt.uint8
 E4M3 = mybir.dt.float8_e4m3fn_x4
 E5M2 = mybir.dt.float8_e5m2_x4
-COPY = mybir.ActivationFunctionType.Copy
 MULT = mybir.AluOpType.mult
 
 
@@ -36,58 +35,66 @@ def tile_veralayer_pa_v_kernel(tc, x, A, B, d_A, d_B, z1, grad_out, out_0, out_1
         warm = sb("warm", [P, 8], F32)
         vec_raw = sb("vec_raw", [P, 512], BF16)
         vec = sb("vec", [P, 512], F32)
+        sel = sb("sel", [P, P], BF16)
         db = sb("db", [P, PASSES, 4], BF16)
-        da = sb("da", [P, 4], F32)
-        g_raw = [[sb("g_raw%d%d" % (f, jj), [P, 2, 1024], BF16) for jj in range(2)] for f in range(2)]
+        da = sb("da", [P, R], F32)
+        g_raw0 = [sb("g_raw0%d" % f, [P, 2, 1024], BF16) for f in range(2)]
+        g_raw1 = sb("g_raw1", [P, 2, DO], BF16)
         b_raw = [sb("b_raw%d" % g, [P, 4, R], BF16) for g in range(PASSES)]
-        a_raw = [sb("a_raw%d" % h, [P, 4, 1024], BF16) for h in range(2)]
-        x_raw = sb("x_raw", [P, 4, DI], BF16)
-        dz2_g = sb("dz2_g", [P, PASSES, T, 4], BF16)
-        dz2_c = sb("dz2_c", [P, PASSES, T], U32)
-        dz2_s = sb("dz2_s", [P, PASSES, T], U8)
+        x_raw = [sb("x_raw%d" % h, [P, 4, 1024], BF16) for h in range(2)]
+        a_raw = sb("a_raw", [P, 4, DI], BF16)
+        dz2_g = sb("dz2_g", [P, 2, PASSES, 256, 4], BF16)
+        dz2_c = sb("dz2_c", [P, 2, PASSES, 256], U32)
+        dz2_s = sb("dz2_s", [P, 2, PASSES, 256], U8)
         b_g = [sb("b_g%d" % g, [P, R, 4], BF16) for g in range(PASSES)]
         b_c = sb("b_c", [P, PASSES, R], U32)
         b_s = sb("b_s", [P, PASSES, R], U8)
         w_g = [sb("w_g%d" % k, [P, 512, 4], BF16) for k in range(3)]
-        a_c = sb("a_c", [P, DI], U32)
-        a_s = sb("a_s", [P, DI], U8)
         x_c = sb("x_c", [P, DI], U32)
         x_s = sb("x_s", [P, DI], U8)
-        d_t = sb("d_t", [P, 4, T], BF16)
-        dr_g = sb("dr_g", [P, T, 4], BF16)
-        dr_c = sb("dr_c", [P, T], U32)
-        dr_s = sb("dr_s", [P, T], U8)
+        a_c = sb("a_c", [P, DI], U32)
+        a_s = sb("a_s", [P, DI], U8)
+        d_t = sb("d_t", [P, 4, R], BF16)
         dt_g = sb("dt_g", [P, R, 4], BF16)
         dt_c = sb("dt_c", [P, R], U32)
         dt_s = sb("dt_s", [P, R], U8)
+        dr_g = sb("dr_g", [P, T, 4], BF16)
+        dr_c = sb("dr_c", [P, T], U32)
+        dr_s = sb("dr_s", [P, T], U8)
 
-        g_v = grad_out.rearrange("b s w -> s b w")
+        nc.vector.memset(vec_raw[:], 0.0)
+        nc.scalar.dma_start(out=vec_raw[0:4, :], in_=d_B.rearrange("(g w) -> g w", g=4))
+        nc.scalar.dma_start(out=vec_raw[32:33, :], in_=d_A.rearrange("(g w) -> g w", g=1))
+        g_v = grad_out.rearrange("b s w -> (b s) w").rearrange("(p j) w -> p j w", j=4)
+        x_v = x.rearrange("b s w -> (b s) w").rearrange("(p j) w -> p j w", j=4)
+        a_v = A.rearrange("(p j) w -> p j w", j=4)
 
-        def load_g(f, jj):
-            nc.sync.dma_start(out=g_raw[f][jj][:], in_=g_v[:, 2 * jj : 2 * jj + 2, 1024 * f : 1024 * (f + 1)])
+        def load_g0(f):
+            nc.sync.dma_start(out=g_raw0[f][:], in_=g_v[:, 0:2, 1024 * f : 1024 * (f + 1)])
+
+        def load_g1(f):
+            cols = slice(1024 * f, 1024 * (f + 1))
+            nc.sync.dma_start(out=g_raw1[:, :, cols], in_=g_v[:, 2:4, cols])
 
         def load_b(g):
             nc.sync.dma_start(out=b_raw[g][:], in_=B[512 * g : 512 * (g + 1), :].rearrange("(p j) r -> p j r", j=4))
 
-        nc.vector.memset(vec_raw[:], 0.0)
-        nc.sync.dma_start(out=vec_raw[0:4, :], in_=d_B.rearrange("(g w) -> g w", g=4))
-        nc.sync.dma_start(out=vec_raw[4:5, :], in_=d_A.rearrange("(g w) -> g w", g=1))
-        load_g(0, 0)
+        load_g0(0)
         load_b(0)
-        load_g(0, 1)
-        load_g(1, 0)
+        load_g0(1)
         load_b(1)
-        load_g(1, 1)
+        load_g1(0)
         load_b(2)
+        load_g1(1)
         load_b(3)
-        a_v = A.rearrange("(p j) w -> p j w", j=4)
-        x_v = x.rearrange("b s w -> (b s) w").rearrange("(p j) w -> p j w", j=4)
         for h in range(2):
-            nc.sync.dma_start(out=a_raw[h][:], in_=a_v[:, :, 1024 * h : 1024 * (h + 1)])
+            nc.sync.dma_start(out=x_raw[h][:], in_=x_v[:, :, 1024 * h : 1024 * (h + 1)])
         for h in range(2):
-            nc.sync.dma_start(out=x_raw[:, 2 * h : 2 * h + 2, :], in_=x_v[:, 2 * h : 2 * h + 2, :])
+            nc.sync.dma_start(out=a_raw[:, 2 * h : 2 * h + 2, :], in_=a_v[:, 2 * h : 2 * h + 2, :])
 
         make_identity(nc, ident[:])
+        nc.vector.memset(sel[:], 0.0)
+        nc.vector.memset(sel[32:33, :], 1.0)
         nc.vector.memset(warm[:, 0:4], 0.0)
         nc.scalar.copy(out=warm[:, 4:5], in_=warm[:, 0:1])
 
@@ -97,13 +104,11 @@ def tile_veralayer_pa_v_kernel(tc, x, A, B, d_A, d_B, z1, grad_out, out_0, out_1
             else:
                 nc.scalar.copy(out=out, in_=in_)
 
-        def il_b(eng, g, m0, m1):
-            cut = (slice(None), slice(None), slice(m0, m1)) if eng == "v" else (slice(None), slice(m0, m1))
-            copy(
-                eng,
-                b_g[g][:].rearrange("p (t m) j -> p %s j" % ("t m" if eng == "v" else "m t"), t=4)[cut],
-                b_raw[g][:].rearrange("p j (m t) -> p %s j" % ("t m" if eng == "v" else "m t"), t=4)[cut],
-            )
+        def il(eng, dst, src):
+            copy(eng, dst.rearrange("p (c i) t -> p c t i", i=4), src.rearrange("p t (c i) -> p c t i", i=4))
+
+        def il_b(eng, g, c0=0, c1=512):
+            il(eng, b_g[g][:, c0:c1, :], b_raw[g][:, :, c0:c1])
 
         def q_b(g):
             nc.vector.quantize_mx(
@@ -113,19 +118,28 @@ def tile_veralayer_pa_v_kernel(tc, x, A, B, d_A, d_B, z1, grad_out, out_0, out_1
         def bank():
             return psum.tile([P, 512], F32, name="bank")
 
+        abank = bank()
+        nc.tensor.matmul(abank[:], lhsT=sel[:], rhs=vec_raw[:], start=True, stop=True)
+        nc.scalar.copy(out=da[:], in_=abank[:])
+
         nc.vector.tensor_copy(out=vec[:], in_=vec_raw[:])
         vbank = bank()
         for j in range(4):
             nc.tensor.transpose(vbank[:, 128 * j : 128 * (j + 1)], vec[:, j:512:4], ident[:])
-        vview = vbank[:].rearrange("p (j r) -> p r j", j=4)
-        nc.vector.tensor_scalar(out=db[:], in0=vview[:, 0:4, :], scalar1=SCALE, scalar2=None, op0=MULT)
-        nc.vector.tensor_copy(out=da[:], in_=vview[:, 4, :])
+        nc.vector.tensor_scalar(
+            out=db[:],
+            in0=vbank[:].rearrange("p (j r) -> p r j", j=4)[:, 0:4, :],
+            scalar1=SCALE,
+            scalar2=None,
+            op0=MULT,
+        )
 
-        def tr_g(f, jj):
+        def tr_g(jj, f):
             banks = [bank() for gl in range(2)]
             for gl in range(2):
                 for k in range(2):
-                    words = g_raw[f][jj][:, k, :].bitcast(F32)
+                    raw = g_raw0[f][:, k, :] if jj == 0 else g_raw1[:, k, 1024 * f : 1024 * (f + 1)]
+                    words = raw.bitcast(F32)
                     for u in range(2):
                         c0 = 256 * u + 128 * k
                         nc.tensor.transpose(
@@ -133,124 +147,130 @@ def tile_veralayer_pa_v_kernel(tc, x, A, B, d_A, d_B, z1, grad_out, out_0, out_1
                         )
             return banks
 
-        def evac_g(f, jj, banks):
-            for gl in range(2):
-                g = 2 * f + gl
-                nc.vector.tensor_tensor(
-                    out=dz2_g[:, g, 256 * jj : 256 * (jj + 1), :].rearrange("p r (u e) -> p r u e", u=2),
-                    in0=banks[gl][:].bitcast(BF16).rearrange("p (u r e) -> p r u e", u=2, e=2),
-                    in1=db[:, g, :].rearrange("p (u e) -> p u e", u=2).unsqueeze(1).to_broadcast([P, 256, 2, 2]),
-                    op=MULT,
-                )
-
-        def q_g(g):
-            nc.vector.quantize_mx(
-                out=dz2_c[:, g, :].bitcast(E5M2),
-                scales=dz2_s[:, g, :],
-                in_=dz2_g[:, g, :, :].rearrange("p c j -> p (c j)"),
+        def evac_g(jj, f, gl, banks):
+            g = 2 * f + gl
+            nc.vector.tensor_tensor(
+                out=dz2_g[:, jj, g, :, :].rearrange("p r (u e) -> p r u e", u=2),
+                in0=banks[gl][:].bitcast(BF16).rearrange("p (u r e) -> p r u e", u=2, e=2),
+                in1=db[:, g, :].rearrange("p (u e) -> p u e", u=2).unsqueeze(1).to_broadcast([P, 256, 2, 2]),
+                op=MULT,
             )
 
-        def mx_dh(g):
-            for t in range(4):
+        def q_g(jj, f):
+            gs = slice(2 * f, 2 * f + 2)
+            nc.vector.quantize_mx(
+                out=dz2_c[:, jj, gs, :].rearrange("p g r -> p (g r)").bitcast(E5M2),
+                scales=dz2_s[:, jj, gs, :].rearrange("p g r -> p (g r)"),
+                in_=dz2_g[:, jj, gs, :, :].rearrange("p g r j -> p (g r j)"),
+            )
+
+        def mx_dh(g, js):
+            for j in js:
+                cols = slice(128 * (j % 2), 128 * (j % 2 + 1))
                 nc.tensor.matmul_mx(
-                    out=acc[t][:],
-                    lhsT=b_c[:, g, 128 * t : 128 * (t + 1)].bitcast(E4M3),
-                    lhsT_scale=b_s[:, g, 128 * t : 128 * (t + 1)],
-                    rhs=dz2_c[:, g, :].bitcast(E5M2),
-                    rhs_scale=dz2_s[:, g, :],
+                    out=acc[j][:],
+                    lhsT=dz2_c[:, j // 2, g, cols].bitcast(E5M2),
+                    lhsT_scale=dz2_s[:, j // 2, g, cols],
+                    rhs=b_c[:, g, :].bitcast(E4M3),
+                    rhs_scale=b_s[:, g, :],
                     start=(g == 0),
                     stop=(g == PASSES - 1),
                 )
 
-        def il(eng, dst, src):
-            copy(eng, dst.rearrange("p (c i) t -> p c t i", i=4), src.rearrange("p t (c i) -> p c t i", i=4))
-
         def il_w(eng, k, c0=0, c1=512):
-            raw = a_raw[k // 2] if k < 4 else x_raw
+            raw = x_raw[k // 2] if k < 4 else a_raw
             base = 512 * (k % 2) if k < 4 else 512 * (k - 4)
             il(eng, w_g[k % 3][:, c0:c1, :], raw[:, :, base + c0 : base + c1])
 
         def q_w(k):
-            c, s = (a_c, a_s) if k < 4 else (x_c, x_s)
+            c, s = (x_c, x_s) if k < 4 else (a_c, a_s)
             cols = slice(512 * (k % 4), 512 * (k % 4 + 1))
             nc.vector.quantize_mx(
                 out=c[:, cols].bitcast(E4M3), scales=s[:, cols], in_=w_g[k % 3][:].rearrange("p c j -> p (c j)")
             )
 
-        def q_dr(h):
+        def evac_dh(j, h):
+            cols = slice(256 * h, 256 * (h + 1))
+            nc.vector.tensor_tensor(out=d_t[:, j, cols], in0=acc[j][:, cols], in1=da[:, cols], op=MULT)
+
+        def q_dt(h):
             cols = slice(256 * h, 256 * (h + 1))
             nc.vector.quantize_mx(
-                out=dr_c[:, cols].bitcast(E5M2), scales=dr_s[:, cols], in_=dr_g[:, cols, :].rearrange("p c j -> p (c j)")
+                out=dt_c[:, cols].bitcast(E5M2), scales=dt_s[:, cols], in_=dt_g[:, cols, :].rearrange("p c j -> p (c j)")
             )
 
-        bl0 = tr_g(0, 0)
-        il_b("s", 0, 64, 128)
-        evac_g(0, 0, bl0)
-        il_b("v", 0, 0, 64)
-        bl1 = tr_g(0, 1)
-        evac_g(0, 1, bl1)
+        b00 = tr_g(0, 0)
+        il_b("v", 0)
+        evac_g(0, 0, 0, b00)
+        evac_g(0, 0, 1, b00)
         q_b(0)
-        q_g(0)
-        il_b("s", 1, 0, 128)
-        br0 = tr_g(1, 0)
-        q_g(1)
-        evac_g(1, 0, br0)
-        br1 = tr_g(1, 1)
+        b01 = tr_g(0, 1)
+        il_b("s", 1)
+        evac_g(0, 1, 0, b01)
+        q_g(0, 0)
+        evac_g(0, 1, 1, b01)
         q_b(1)
-        evac_g(1, 1, br1)
-        acc = [bank() for t in range(4)]
-        mx_dh(0)
-        mx_dh(1)
-        il_b("s", 2, 0, 128)
-        il_b("s", 3, 0, 128)
-        q_g(2)
-        q_g(3)
+        b10 = tr_g(1, 0)
+        evac_g(1, 0, 0, b10)
+        q_g(0, 1)
+        evac_g(1, 0, 1, b10)
+        il_b("s", 2)
+        b11 = tr_g(1, 1)
+        acc = [bank() for j in range(4)]
+        mx_dh(0, (0, 1))
+        mx_dh(1, (0, 1))
+        evac_g(1, 1, 0, b11)
+        q_g(1, 0)
+        evac_g(1, 1, 1, b11)
+        mx_dh(0, (2, 3))
+        mx_dh(1, (2, 3))
         q_b(2)
-        mx_dh(2)
-        q_b(3)
-        mx_dh(3)
-        il_w("s", 0, 256, 512)
+        mx_dh(2, (0, 1))
+        il_b("s", 3)
         il_w("v", 0, 0, 256)
-        for t in range(4):
-            if t in (0, 2):
-                nc.scalar.activation(out=d_t[:, t, :], in_=acc[t][:], func=COPY, scale=da[:, t : t + 1])
-            else:
-                nc.vector.tensor_scalar(
-                    out=d_t[:, t, :], in0=acc[t][:], scalar1=da[:, t : t + 1], scalar2=None, op0=MULT
-                )
-        il("v", dr_g[:, 0:320, :], d_t[:, :, 0:320])
-        il("s", dr_g[:, 320:512, :], d_t[:, :, 320:512])
+        q_g(1, 1)
+        mx_dh(2, (2, 3))
+        q_b(3)
+        mx_dh(3, range(4))
+        il_w("s", 0, 256, 512)
+        il_w("s", 1, 0, 384)
         q_w(0)
-        q_dr(0)
-        il_w("v", 1, 0, 384)
+        for j in range(4):
+            evac_dh(j, 0)
+        evac_dh(0, 1)
+        il("v", dt_g[:, 0:128, :], d_t[:, :, 0:128])
+        il("s", dt_g[:, 128:256, :], d_t[:, :, 128:256])
         il_w("s", 1, 384, 512)
-        q_dr(1)
+        evac_dh(1, 1)
+        q_dt(0)
+        evac_dh(2, 1)
+        q_w(1)
+        evac_dh(3, 1)
+        il("v", dt_g[:, 256:512, :], d_t[:, :, 256:512])
+        il_w("v", 2, 0, 128)
+        q_dt(1)
+        il_w("v", 2, 128, 512)
 
-        def tr_d():
-            banks = [bank() for k in range(2)]
-            words = d_t[:].rearrange("p t r -> p (t r)").bitcast(F32)
-            for k in range(2):
+        def tr_d(k):
+            dbanks.append(bank())
+            for i in range(2):
+                words = d_t[:, 2 * k + i, :].bitcast(F32)
                 for u in range(2):
-                    for i in range(2):
-                        t = 2 * k + i
-                        c0 = 256 * u + 128 * i
-                        nc.tensor.transpose(
-                            banks[k][:, c0 : c0 + 128], words[:, 256 * t + u : 256 * (t + 1) : 2], ident[:]
-                        )
-            return banks
+                    c0 = 256 * u + 128 * i
+                    nc.tensor.transpose(dbanks[k][:, c0 : c0 + 128], words[:, u:256:2], ident[:])
 
-        def evac_d(banks, k):
-            nc.vector.tensor_copy(
-                out=dt_g[:, 256 * k : 256 * (k + 1), :].rearrange("p c j -> p (c j)").bitcast(F32).rearrange("p (c u) -> p c u", u=2),
-                in_=banks[k][:].rearrange("p (u c) -> p c u", u=2),
+        def evac_d(k):
+            nc.scalar.copy(
+                out=dr_g[:, 256 * k : 256 * (k + 1), :].rearrange("p c j -> p (c j)").bitcast(F32).rearrange("p (c u) -> p c u", u=2),
+                in_=dbanks[k][:].rearrange("p (u c) -> p c u", u=2),
             )
 
-        def q_dt():
-            nc.vector.quantize_mx(out=dt_c[:].bitcast(E5M2), scales=dt_s[:], in_=dt_g[:].rearrange("p c j -> p (c j)"))
+        def q_dr():
+            nc.vector.quantize_mx(out=dr_c[:].bitcast(E5M2), scales=dr_s[:], in_=dr_g[:].rearrange("p c j -> p (c j)"))
 
         def mx_out(ps, chunk, mt):
-            lc, ls = (dr_c, dr_s) if chunk < 4 else (dt_c, dt_s)
-            rc, rs = (a_c, a_s) if chunk < 4 else (x_c, x_s)
+            lc, ls = (dt_c, dt_s) if chunk < 4 else (dr_c, dr_s)
+            rc, rs = (x_c, x_s) if chunk < 4 else (a_c, a_s)
             rows = slice(128 * mt, 128 * (mt + 1))
             cols = slice(512 * (chunk % 4), 512 * (chunk % 4 + 1))
             nc.tensor.matmul_mx(
@@ -263,69 +283,65 @@ def tile_veralayer_pa_v_kernel(tc, x, A, B, d_A, d_B, z1, grad_out, out_0, out_1
                 stop=True,
             )
 
-        out1_v = out_1.rearrange("(m t) n -> m t n", t=4)
-        out0_v = out_0.rearrange("b s w -> s b w")
-        on_vector = {25, 27, 29, 31}
+        out0_v = out_0.rearrange("b s w -> (b s) w").rearrange("(m j) w -> m j w", j=4)
+        out1_v = out_1.rearrange("(t m) n -> m t n", t=4)
         dbanks = []
 
-        def vector_work(n):
-            if n == 1:
-                q_w(1)
-                il_w("v", 2)
-            elif n == 3:
-                q_w(2)
+        on_vector = {8, 25, 26, 27, 28}
+
+        def extra_work(n):
+            if n == 3:
                 il_w("v", 3)
+                q_w(2)
+                tr_d(0)
             elif n == 5:
-                dbanks.extend(tr_d())
                 q_w(3)
+                tr_d(1)
             elif n == 7:
-                evac_d(dbanks, 0)
-                evac_d(dbanks, 1)
-                il_w("v", 4)
-                q_dt()
+                evac_d(0)
             elif n == 9:
+                evac_d(1)
+            elif n == 8:
+                il_w("v", 4)
+            elif n == 10:
+                q_dr()
                 q_w(4)
                 il_w("v", 5)
-            elif n == 13:
+            elif n == 15:
                 q_w(5)
                 il_w("v", 6)
-            elif n == 18:
+            elif n == 19:
                 q_w(6)
                 il_w("v", 7)
-            elif n == 21:
+            elif n == 22:
                 q_w(7)
 
         def emit(n, chunk, mt, dst):
             ps = bank()
             mx_out(ps, chunk, mt)
             copy("v" if n in on_vector else "s", dst, ps[:])
-            vector_work(n)
+            extra_work(n)
 
-        out0_v = out_0.rearrange("b s w -> s b w")
         n = 0
         for unit in range(4):
-            view = out0_v if unit < 2 else out1_v
+            view = out1_v if unit < 2 else out0_v
             c0 = 1024 * (unit % 2)
-            for q in range(4):
-                st = stage.tile([P, 2, 512], F32, name="st")
-                if unit % 2 == 0:
-                    chunk, m0 = 2 * unit + q // 2, 2 * (q % 2)
-                    cols = slice(c0 + 512 * (q // 2), c0 + 512 * (q // 2 + 1))
-                    for i in range(2):
-                        emit(n, chunk, m0 + i, st[:, i, :])
+            for half in range(2):
+                single = (unit, half) in ((0, 0), (3, 1))
+                by_rows = unit in (0, 3)
+                sts = [stage.tile([P, 2, 512], F32, name="st") for k in range(2)]
+                for a in range(2):
+                    for b in range(2):
+                        k, i = (b, a) if single else (a, b)
+                        mt, side = (2 * half + k, i) if by_rows else (2 * k + i, half)
+                        emit(n, 2 * unit + side, mt, sts[k][:, i, :])
                         n += 1
-                        if n <= 2:
-                            nc.sync.dma_start(out=view[:, m0 + i, cols], in_=st[:, i, :])
-                    if n > 2:
-                        nc.sync.dma_start(out=view[:, m0 : m0 + 2, cols], in_=st[:])
-                else:
-                    for i in range(2):
-                        emit(n, 2 * unit + i, q, st[:, i, :])
-                        n += 1
-                        if n > 30:
-                            cols = slice(c0 + 512 * i, c0 + 512 * (i + 1))
-                            nc.sync.dma_start(out=view[:, q, cols], in_=st[:, i, :])
-                    if n <= 30:
-                        nc.sync.dma_start(
-                            out=view[:, q, c0 : c0 + 1024], in_=st[:].rearrange("p i w -> p (i w)")
-                        )
+                        cols = slice(c0 + 512 * side, c0 + 512 * (side + 1))
+                        if single:
+                            nc.sync.dma_start(out=view[:, mt, cols], in_=sts[k][:, i, :])
+                        elif by_rows and b == 1:
+                            nc.sync.dma_start(
+                                out=view[:, mt, c0 : c0 + 1024], in_=sts[k][:].rearrange("p i w -> p (i w)")
+                            )
+                        elif b == 1:
+                            nc.sync.dma_start(out=view[:, 2 * k : 2 * k + 2, cols], in_=sts[k][:])

from contextlib import ExitStack

import concourse.mybir as mybir
from concourse.masks import make_identity

T, DI, DO, R = 512, 2048, 2048, 512
P = 128
PASSES = DO // 512
SCALE = 0.125

FLOPS = 3 * 2 * T * DO * R
BYTES = 2 * (T * DI + R * DI + DO * R + T * DO + R + DO) + 4 * (T * DI + R * DI)

F32 = mybir.dt.float32
BF16 = mybir.dt.bfloat16
U32 = mybir.dt.uint32
U8 = mybir.dt.uint8
E4M3 = mybir.dt.float8_e4m3fn_x4
E5M2 = mybir.dt.float8_e5m2_x4
MULT = mybir.AluOpType.mult


def tile_veralayer_pa_v_kernel(tc, x, A, B, d_A, d_B, z1, grad_out, out_0, out_1):
    nc = tc.nc
    with ExitStack() as ctx:
        keep = ctx.enter_context(tc.tile_pool(name="keep", bufs=1))
        stage = ctx.enter_context(tc.tile_pool(name="stage", bufs=6))
        psum = ctx.enter_context(tc.psum_pool(name="psum", bufs=8))
        ctx.enter_context(tc.manual_schedule())

        def sb(name, shape, dtype):
            return keep.tile(shape, dtype, name=name, align_bytes=64)

        ident = sb("ident", [P, P], F32)
        warm = sb("warm", [P, 8], F32)
        vec_raw = sb("vec_raw", [P, 512], BF16)
        vec = sb("vec", [P, 512], F32)
        sel = sb("sel", [P, P], BF16)
        db = sb("db", [P, PASSES, 4], BF16)
        da = sb("da", [P, R], F32)
        g_raw0 = [sb("g_raw0%d" % f, [P, 2, 1024], BF16) for f in range(2)]
        g_raw1 = sb("g_raw1", [P, 2, DO], BF16)
        b_raw = [sb("b_raw%d" % g, [P, 4, R], BF16) for g in range(PASSES)]
        x_raw = [sb("x_raw%d" % h, [P, 4, 1024], BF16) for h in range(2)]
        a_raw = sb("a_raw", [P, 4, DI], BF16)
        dz2_g = sb("dz2_g", [P, 2, PASSES, 256, 4], BF16)
        dz2_c = sb("dz2_c", [P, 2, PASSES, 256], U32)
        dz2_s = sb("dz2_s", [P, 2, PASSES, 256], U8)
        b_g = [sb("b_g%d" % g, [P, R, 4], BF16) for g in range(PASSES)]
        b_c = sb("b_c", [P, PASSES, R], U32)
        b_s = sb("b_s", [P, PASSES, R], U8)
        w_g = [sb("w_g%d" % k, [P, 512, 4], BF16) for k in range(3)]
        x_c = sb("x_c", [P, DI], U32)
        x_s = sb("x_s", [P, DI], U8)
        a_c = sb("a_c", [P, DI], U32)
        a_s = sb("a_s", [P, DI], U8)
        d_t = sb("d_t", [P, 4, R], BF16)
        dt_g = sb("dt_g", [P, R, 4], BF16)
        dt_c = sb("dt_c", [P, R], U32)
        dt_s = sb("dt_s", [P, R], U8)
        dr_g = sb("dr_g", [P, T, 4], BF16)
        dr_c = sb("dr_c", [P, T], U32)
        dr_s = sb("dr_s", [P, T], U8)

        nc.vector.memset(vec_raw[:], 0.0)
        nc.scalar.dma_start(out=vec_raw[0:4, :], in_=d_B.rearrange("(g w) -> g w", g=4))
        nc.scalar.dma_start(out=vec_raw[32:33, :], in_=d_A.rearrange("(g w) -> g w", g=1))
        g_v = grad_out.rearrange("b s w -> (b s) w").rearrange("(p j) w -> p j w", j=4)
        x_v = x.rearrange("b s w -> (b s) w").rearrange("(p j) w -> p j w", j=4)
        a_v = A.rearrange("(p j) w -> p j w", j=4)

        def load_g0(f):
            nc.sync.dma_start(out=g_raw0[f][:], in_=g_v[:, 0:2, 1024 * f : 1024 * (f + 1)])

        def load_g1(f):
            cols = slice(1024 * f, 1024 * (f + 1))
            nc.sync.dma_start(out=g_raw1[:, :, cols], in_=g_v[:, 2:4, cols])

        def load_b(g):
            nc.sync.dma_start(out=b_raw[g][:], in_=B[512 * g : 512 * (g + 1), :].rearrange("(p j) r -> p j r", j=4))

        load_g0(0)
        load_b(0)
        load_g0(1)
        load_b(1)
        load_g1(0)
        load_b(2)
        load_g1(1)
        load_b(3)
        for h in range(2):
            nc.sync.dma_start(out=x_raw[h][:], in_=x_v[:, :, 1024 * h : 1024 * (h + 1)])
        for h in range(2):
            nc.sync.dma_start(out=a_raw[:, 2 * h : 2 * h + 2, :], in_=a_v[:, 2 * h : 2 * h + 2, :])

        make_identity(nc, ident[:])
        nc.vector.memset(sel[:], 0.0)
        nc.vector.memset(sel[32:33, :], 1.0)
        nc.vector.memset(warm[:, 0:4], 0.0)
        nc.scalar.copy(out=warm[:, 4:5], in_=warm[:, 0:1])

        def copy(eng, out, in_):
            if eng == "v":
                nc.vector.tensor_copy(out=out, in_=in_)
            else:
                nc.scalar.copy(out=out, in_=in_)

        def il(eng, dst, src):
            copy(eng, dst.rearrange("p (c i) t -> p c t i", i=4), src.rearrange("p t (c i) -> p c t i", i=4))

        def il_b(eng, g, c0=0, c1=512):
            il(eng, b_g[g][:, c0:c1, :], b_raw[g][:, :, c0:c1])

        def q_b(g):
            nc.vector.quantize_mx(
                out=b_c[:, g, :].bitcast(E4M3), scales=b_s[:, g, :], in_=b_g[g][:].rearrange("p c j -> p (c j)")
            )

        def bank():
            return psum.tile([P, 512], F32, name="bank")

        abank = bank()
        nc.tensor.matmul(abank[:], lhsT=sel[:], rhs=vec_raw[:], start=True, stop=True)
        nc.scalar.copy(out=da[:], in_=abank[:])

        nc.vector.tensor_copy(out=vec[:], in_=vec_raw[:])
        vbank = bank()
        for j in range(4):
            nc.tensor.transpose(vbank[:, 128 * j : 128 * (j + 1)], vec[:, j:512:4], ident[:])
        nc.vector.tensor_scalar(
            out=db[:],
            in0=vbank[:].rearrange("p (j r) -> p r j", j=4)[:, 0:4, :],
            scalar1=SCALE,
            scalar2=None,
            op0=MULT,
        )

        def tr_g(jj, f):
            banks = [bank() for gl in range(2)]
            for gl in range(2):
                for k in range(2):
                    raw = g_raw0[f][:, k, :] if jj == 0 else g_raw1[:, k, 1024 * f : 1024 * (f + 1)]
                    words = raw.bitcast(F32)
                    for u in range(2):
                        c0 = 256 * u + 128 * k
                        nc.tensor.transpose(
                            banks[gl][:, c0 : c0 + 128], words[:, 256 * gl + u : 256 * (gl + 1) : 2], ident[:]
                        )
            return banks

        def evac_g(jj, f, gl, banks):
            g = 2 * f + gl
            nc.vector.tensor_tensor(
                out=dz2_g[:, jj, g, :, :].rearrange("p r (u e) -> p r u e", u=2),
                in0=banks[gl][:].bitcast(BF16).rearrange("p (u r e) -> p r u e", u=2, e=2),
                in1=db[:, g, :].rearrange("p (u e) -> p u e", u=2).unsqueeze(1).to_broadcast([P, 256, 2, 2]),
                op=MULT,
            )

        def q_g(jj, f):
            gs = slice(2 * f, 2 * f + 2)
            nc.vector.quantize_mx(
                out=dz2_c[:, jj, gs, :].rearrange("p g r -> p (g r)").bitcast(E5M2),
                scales=dz2_s[:, jj, gs, :].rearrange("p g r -> p (g r)"),
                in_=dz2_g[:, jj, gs, :, :].rearrange("p g r j -> p (g r j)"),
            )

        def mx_dh(g, js):
            for j in js:
                cols = slice(128 * (j % 2), 128 * (j % 2 + 1))
                nc.tensor.matmul_mx(
                    out=acc[j][:],
                    lhsT=dz2_c[:, j // 2, g, cols].bitcast(E5M2),
                    lhsT_scale=dz2_s[:, j // 2, g, cols],
                    rhs=b_c[:, g, :].bitcast(E4M3),
                    rhs_scale=b_s[:, g, :],
                    start=(g == 0),
                    stop=(g == PASSES - 1),
                )

        def il_w(eng, k, c0=0, c1=512):
            raw = x_raw[k // 2] if k < 4 else a_raw
            base = 512 * (k % 2) if k < 4 else 512 * (k - 4)
            il(eng, w_g[k % 3][:, c0:c1, :], raw[:, :, base + c0 : base + c1])

        def q_w(k):
            c, s = (x_c, x_s) if k < 4 else (a_c, a_s)
            cols = slice(512 * (k % 4), 512 * (k % 4 + 1))
            nc.vector.quantize_mx(
                out=c[:, cols].bitcast(E4M3), scales=s[:, cols], in_=w_g[k % 3][:].rearrange("p c j -> p (c j)")
            )

        def evac_dh(j, h):
            cols = slice(256 * h, 256 * (h + 1))
            nc.vector.tensor_tensor(out=d_t[:, j, cols], in0=acc[j][:, cols], in1=da[:, cols], op=MULT)

        def q_dt(h):
            cols = slice(256 * h, 256 * (h + 1))
            nc.vector.quantize_mx(
                out=dt_c[:, cols].bitcast(E5M2), scales=dt_s[:, cols], in_=dt_g[:, cols, :].rearrange("p c j -> p (c j)")
            )

        b00 = tr_g(0, 0)
        il_b("v", 0)
        evac_g(0, 0, 0, b00)
        evac_g(0, 0, 1, b00)
        q_b(0)
        b01 = tr_g(0, 1)
        il_b("s", 1)
        evac_g(0, 1, 0, b01)
        q_g(0, 0)
        evac_g(0, 1, 1, b01)
        q_b(1)
        b10 = tr_g(1, 0)
        evac_g(1, 0, 0, b10)
        q_g(0, 1)
        evac_g(1, 0, 1, b10)
        il_b("s", 2)
        b11 = tr_g(1, 1)
        acc = [bank() for j in range(4)]
        mx_dh(0, (0, 1))
        mx_dh(1, (0, 1))
        evac_g(1, 1, 0, b11)
        q_g(1, 0)
        evac_g(1, 1, 1, b11)
        mx_dh(0, (2, 3))
        mx_dh(1, (2, 3))
        q_b(2)
        mx_dh(2, (0, 1))
        il_b("s", 3)
        il_w("v", 0, 0, 256)
        q_g(1, 1)
        mx_dh(2, (2, 3))
        q_b(3)
        mx_dh(3, range(4))
        il_w("s", 0, 256, 512)
        il_w("s", 1, 0, 384)
        q_w(0)
        for j in range(4):
            evac_dh(j, 0)
        evac_dh(0, 1)
        il("v", dt_g[:, 0:128, :], d_t[:, :, 0:128])
        il("s", dt_g[:, 128:256, :], d_t[:, :, 128:256])
        il_w("s", 1, 384, 512)
        evac_dh(1, 1)
        q_dt(0)
        evac_dh(2, 1)
        q_w(1)
        evac_dh(3, 1)
        il("v", dt_g[:, 256:512, :], d_t[:, :, 256:512])
        il_w("v", 2, 0, 128)
        q_dt(1)
        il_w("v", 2, 128, 512)

        def tr_d(k):
            dbanks.append(bank())
            for i in range(2):
                words = d_t[:, 2 * k + i, :].bitcast(F32)
                for u in range(2):
                    c0 = 256 * u + 128 * i
                    nc.tensor.transpose(dbanks[k][:, c0 : c0 + 128], words[:, u:256:2], ident[:])

        def evac_d(k):
            nc.scalar.copy(
                out=dr_g[:, 256 * k : 256 * (k + 1), :].rearrange("p c j -> p (c j)").bitcast(F32).rearrange("p (c u) -> p c u", u=2),
                in_=dbanks[k][:].rearrange("p (u c) -> p c u", u=2),
            )

        def q_dr():
            nc.vector.quantize_mx(out=dr_c[:].bitcast(E5M2), scales=dr_s[:], in_=dr_g[:].rearrange("p c j -> p (c j)"))

        def mx_out(ps, chunk, mt):
            lc, ls = (dt_c, dt_s) if chunk < 4 else (dr_c, dr_s)
            rc, rs = (x_c, x_s) if chunk < 4 else (a_c, a_s)
            rows = slice(128 * mt, 128 * (mt + 1))
            cols = slice(512 * (chunk % 4), 512 * (chunk % 4 + 1))
            nc.tensor.matmul_mx(
                out=ps[:],
                lhsT=lc[:, rows].bitcast(E5M2),
                lhsT_scale=ls[:, rows],
                rhs=rc[:, cols].bitcast(E4M3),
                rhs_scale=rs[:, cols],
                start=True,
                stop=True,
            )

        out0_v = out_0.rearrange("b s w -> (b s) w").rearrange("(m j) w -> m j w", j=4)
        out1_v = out_1.rearrange("(t m) n -> m t n", t=4)
        dbanks = []

        on_vector = {8, 25, 26, 27, 28}

        def extra_work(n):
            if n == 3:
                il_w("v", 3)
                q_w(2)
                tr_d(0)
            elif n == 5:
                q_w(3)
                tr_d(1)
            elif n == 7:
                evac_d(0)
            elif n == 9:
                evac_d(1)
            elif n == 8:
                il_w("v", 4)
            elif n == 10:
                q_dr()
                q_w(4)
                il_w("v", 5)
            elif n == 15:
                q_w(5)
                il_w("v", 6)
            elif n == 19:
                q_w(6)
                il_w("v", 7)
            elif n == 22:
                q_w(7)

        def emit(n, chunk, mt, dst):
            ps = bank()
            mx_out(ps, chunk, mt)
            copy("v" if n in on_vector else "s", dst, ps[:])
            extra_work(n)

        n = 0
        for unit in range(4):
            view = out1_v if unit < 2 else out0_v
            c0 = 1024 * (unit % 2)
            for half in range(2):
                single = (unit, half) in ((0, 0), (3, 1))
                by_rows = unit in (0, 3)
                sts = [stage.tile([P, 2, 512], F32, name="st") for k in range(2)]
                for a in range(2):
                    for b in range(2):
                        k, i = (b, a) if single else (a, b)
                        mt, side = (2 * half + k, i) if by_rows else (2 * k + i, half)
                        emit(n, 2 * unit + side, mt, sts[k][:, i, :])
                        n += 1
                        cols = slice(c0 + 512 * side, c0 + 512 * (side + 1))
                        if single:
                            nc.sync.dma_start(out=view[:, mt, cols], in_=sts[k][:, i, :])
                        elif by_rows and b == 1:
                            nc.sync.dma_start(
                                out=view[:, mt, c0 : c0 + 1024], in_=sts[k][:].rearrange("p i w -> p (i w)")
                            )
                        elif b == 1:
                            nc.sync.dma_start(out=view[:, 2 * k : 2 * k + 2, cols], in_=sts[k][:])
